import numpy as np
import ml_dtypes


def mxq(x, axis, fmt="e4m3"):
    dtype, down = {"e4m3": (ml_dtypes.float8_e4m3fn, 7), "e5m2": (ml_dtypes.float8_e5m2, 14)}[fmt]
    v = np.moveaxis(np.asarray(x, np.float32).astype(ml_dtypes.bfloat16).astype(np.float64), axis, -1)
    blocks = v.reshape(v.shape[:-1] + (-1, 32))
    amax = np.abs(blocks).max(-1, keepdims=True)
    byte = np.maximum(np.where(amax > 0, np.frexp(amax)[1] - 1 + 127, 0) - down, 1)
    scale = np.exp2(byte - 127.0)
    codes = (blocks / scale).astype(np.float32).astype(dtype).astype(np.float64)
    return np.moveaxis((codes * scale).reshape(v.shape), -1, axis)


WIDE = False


def mx_kscale(k):
    if not WIDE:
        return np.ones(k)
    levels = np.array([30, -30])
    if k % 512:
        return np.exp2(np.random.permutation(np.resize(levels, k // 32))).repeat(32)
    a = np.empty((k // 512, 16))
    for p in range(k // 512):
        a[p, :8] = np.random.permutation(np.resize(levels, 8))
        for g in range(8):
            far = levels[np.abs(levels - a[p, g]) >= 10]
            a[p, g + 8] = far[np.random.randint(len(far))]
    return np.exp2(a.ravel()).repeat(32)


BF16 = ml_dtypes.bfloat16


def bf(x):
    return np.asarray(x, np.float32).astype(BF16)


def f64(x):
    return np.asarray(x).astype(np.float64)


E2M1 = np.array([0.0, 0.5, 1.0, 1.5, 2.0, 3.0, 4.0, 6.0, -0.0, -0.5, -1.0, -1.5, -2.0, -3.0, -4.0, -6.0])


def pack_weight(w, fmt):
    k, n = w.shape
    w = f64(bf(w)).reshape(k // 32, 32, n)
    amax = np.abs(w).max(1)
    if fmt == "e4m3":
        byte = np.frexp(amax)[1] - 1 + 127 - 7
    else:
        mant, ex = np.frexp(amax / 6.0)
        byte = np.where(mant > 0.5, ex, ex - 1) + 127
    byte = np.clip(np.where(amax > 0, byte, 1), 1, 254)
    scaled = (w * np.exp2(127.0 - byte)[:, None, :]).reshape(k, n).astype(np.float32)
    by_word = np.ascontiguousarray(scaled.reshape(k // 512, 128, 4, n).transpose(0, 1, 3, 2))
    if fmt == "e4m3":
        words = by_word.astype(ml_dtypes.float8_e4m3fn).view(np.uint8)
    else:
        c = by_word.astype(ml_dtypes.float4_e2m1fn).view(np.uint8) & 0xF
        words = c[..., 0::2] | (c[..., 1::2] << 4)
    return np.ascontiguousarray(words), np.ascontiguousarray(byte.astype(np.uint8).reshape(k // 512, 16, n))


def unpack_weight(words, scales, fmt):
    g, p, n, _ = words.shape
    if fmt == "e4m3":
        vals = np.ascontiguousarray(words).view(ml_dtypes.float8_e4m3fn).astype(np.float64)
    else:
        nib = np.empty((g, p, n, 4), np.uint8)
        nib[..., 0::2] = words & 0xF
        nib[..., 1::2] = words >> 4
        vals = E2M1[nib]
    vals = vals * np.repeat(np.exp2(scales.astype(np.float64) - 127.0), 8, axis=1)[..., None]
    return vals.transpose(0, 1, 3, 2).reshape(g * 512, n)

def pack4(w):
    words, scales = pack_weight(w, "e2m1")
    return words.reshape(words.shape[0], 128, -1), scales


def unpack4(words, scales):
    return unpack_weight(words.reshape(words.shape[0], 128, -1, 2), scales, "e2m1")


B, T, C, H, KV, D = 2, 256, 2048, 16, 4, 128
EPS = 1e-5
THETA = 10000.0


def rmsnorm(h, w):
    var = np.mean(np.square(h), axis=-1, keepdims=True)
    return h * (1.0 / np.sqrt(var + EPS)) * w


def rope(h, cos, sin):
    hr = h.reshape(*h.shape[:-1], D // 2, 2)
    a, b = hr[..., 0], hr[..., 1]
    c = cos[None, :, None, :]
    s = sin[None, :, None, :]
    return np.stack([a * c - b * s, a * s + b * c], axis=-1).reshape(h.shape)


def setup_inputs():
    s = mx_kscale(C)
    w_scale = 1.0 / np.sqrt(C)
    inv_freq = 1.0 / (THETA ** (np.arange(0, D, 2) / D))
    angles = np.arange(T)[:, None] * inv_freq[None, :]
    x = bf(np.random.standard_normal((B, T, C)) * s)
    Wq_words, Wq_scales = pack4(np.random.standard_normal((C, H * D)) * w_scale / s[:, None])
    bq = bf(np.random.standard_normal(H * D) * 0.1)
    Wk_words, Wk_scales = pack4(np.random.standard_normal((C, KV * D)) * w_scale / s[:, None])
    bk = bf(np.random.standard_normal(KV * D) * 0.1)
    Wv_words, Wv_scales = pack4(np.random.standard_normal((C, KV * D)) * w_scale / s[:, None])
    bv = bf(np.random.standard_normal(KV * D) * 0.1)
    qn_w = bf(1.0 + 0.1 * np.random.standard_normal(D))
    kn_w = bf(1.0 + 0.1 * np.random.standard_normal(D))
    return {"x": x,
            "Wq_words": Wq_words,
            "Wq_scales": Wq_scales,
            "bq": bq,
            "Wk_words": Wk_words,
            "Wk_scales": Wk_scales,
            "bk": bk,
            "Wv_words": Wv_words,
            "Wv_scales": Wv_scales,
            "bv": bv,
            "qn_w": qn_w,
            "kn_w": kn_w,
            "freqs_cos": bf(np.cos(angles)),
            "freqs_sin": bf(np.sin(angles))}


def reference(x, Wq_words, Wq_scales, bq, Wk_words, Wk_scales, bk, Wv_words, Wv_scales, bv, qn_w, kn_w, freqs_cos, freqs_sin):
    xq = mxq(f64(x), 2, "e5m2")
    q = ((xq @ unpack4(Wq_words, Wq_scales)) + f64(bq)).reshape(B, T, H, D)
    k = ((xq @ unpack4(Wk_words, Wk_scales)) + f64(bk)).reshape(B, T, KV, D)
    v = ((xq @ unpack4(Wv_words, Wv_scales)) + f64(bv)).reshape(B, T, KV, D)
    q = rmsnorm(q, f64(qn_w))
    k = rmsnorm(k, f64(kn_w))
    q = rope(q, f64(freqs_cos), f64(freqs_sin))
    k = rope(k, f64(freqs_cos), f64(freqs_sin))
    return q, k, v

@@ -1,0 +1,319 @@
+from contextlib import ExitStack
+
+import concourse.mybir as mybir
+from concourse.masks import make_identity
+
+B, T, C, H, KV, D = 2, 256, 2048, 16, 4, 128
+EPS = 1e-5
+FLOPS = 2 * B * T * C * (H + 2 * KV) * D
+
+F32 = mybir.dt.float32
+BF16 = mybir.dt.bfloat16
+I32 = mybir.dt.int32
+U32 = mybir.dt.uint32
+U8 = mybir.dt.uint8
+E5M2X4 = mybir.dt.float8_e5m2_x4
+E2M1X4 = mybir.dt.float4_e2m1fn_x4
+ALU = mybir.AluOpType
+ACT = mybir.ActivationFunctionType
+
+P = 128
+TOKENS = B * T
+TILES = TOKENS // P
+K_PASS = 512
+PASSES = C // K_PASS
+NORMED = H + KV
+BLOCK = 512
+HEADS_PER_BLOCK = BLOCK // D
+OPEN_AT_START = 3
+BANKS = 4
+
+
+def tile_llamacausalselfattention_pa_kernel(
+    tc, x, Wq_words, Wq_scales, bq, Wk_words, Wk_scales, bk, Wv_words, Wv_scales, bv,
+    qn_w, kn_w, freqs_cos, freqs_sin, out_0, out_1, out_2,
+):
+    nc = tc.nc
+    x_rows = x.rearrange("b (u p) c -> p (b u) c", p=P)
+    q_rows = out_0.rearrange("b (u p) h d -> p (b u) (h d)", p=P)
+    k_rows = out_1.rearrange("b (u p) h d -> p (b u) (h d)", p=P)
+    v_rows = out_2.rearrange("b (u p) h d -> p (b u) (h d)", p=P)
+
+    with ExitStack() as ctx:
+        keep = ctx.enter_context(tc.tile_pool(name="keep", bufs=1))
+        work = ctx.enter_context(tc.tile_pool(name="work", bufs=4))
+        psum = ctx.enter_context(tc.psum_pool(name="psum", bufs=1))
+        ctx.enter_context(tc.manual_schedule())
+
+        ident_f32 = keep.tile([P, P], F32, name="ident_f32")
+        ident_bf16 = keep.tile([P, P], BF16, name="ident_bf16")
+        vectors = keep.tile([P, D], BF16, name="vectors")
+        trig = keep.tile([P, 3, 2, D // 2], BF16, name="trig")
+        bias_cols = keep.tile([P, NORMED], F32, name="bias_cols")
+        bv_rows = keep.tile([P, BLOCK], BF16, name="bv_rows")
+        x_sb = [[keep.tile([P, 2, K_PASS], BF16, name="x_%d_%d" % (g, a)) for a in range(2)] for g in range(PASSES)]
+        x_grouped = [keep.tile([P, TOKENS, 4], BF16, name="xg_%d" % g, align_bytes=64) for g in range(PASSES)]
+        x_codes = [keep.tile([P, TOKENS], U32, name="xc_%d" % g, align_bytes=64) for g in range(PASSES)]
+        x_scales = [keep.tile([P, TOKENS], U8, name="xs_%d" % g, align_bytes=64) for g in range(PASSES)]
+        words = [keep.tile([P, PASSES, 2 * BLOCK], U8, name="words_%d" % j, align_bytes=64) for j in range(6)]
+        plane_first = keep.tile([P, PASSES, BLOCK], U8, name="plane_first", align_bytes=64)
+        plane_rest = keep.tile([P, PASSES, 3 * BLOCK], U8, name="plane_rest", align_bytes=64)
+        plane_k = keep.tile([P, PASSES, BLOCK], U8, name="plane_k", align_bytes=64)
+        plane_v = keep.tile([P, PASSES, BLOCK], U8, name="plane_v", align_bytes=64)
+        tables = [[keep.tile([P, 2, D // 2, 2], F32, name="table_%d_%d" % (n, e)) for e in range(2)] for n in range(2)]
+
+        def zero_plane(plane):
+            nc.vector.memset(plane[:].rearrange("p g n -> p (g n)").bitcast(I32), 0)
+
+        def load_x(g, a):
+            nc.sync.dma_start(out=x_sb[g][a][:], in_=x_rows[:, 2 * a : 2 * a + 2, K_PASS * g : K_PASS * (g + 1)])
+
+        def load_scales(plane, scales):
+            for q in range(4):
+                nc.sync.dma_start(
+                    out=plane[32 * q : 32 * q + 4, :, :].bitcast(I32),
+                    in_=scales[:, 4 * q : 4 * q + 4, :].rearrange("g r n -> r g n").bitcast(I32),
+                )
+
+        def load_words(j, src, passes):
+            nc.sync.dma_start(
+                out=words[j][:, passes, :].bitcast(I32),
+                in_=src[passes, :, :].rearrange("g p n -> p g n").bitcast(I32),
+            )
+
+        def q_words(j):
+            return Wq_words[:, :, 2 * BLOCK * j : 2 * BLOCK * (j + 1)]
+
+        zero_plane(plane_first)
+        nc.vector.memset(vectors[:], 0.0)
+        make_identity(nc, ident_f32[:])
+        nc.gpsimd.dma_start(out=vectors[0:H, :], in_=bq.rearrange("(h d) -> h d", d=D))
+        nc.gpsimd.dma_start(out=vectors[H:NORMED, :], in_=bk.rearrange("(h d) -> h d", d=D))
+        nc.gpsimd.dma_start(out=vectors[NORMED : NORMED + 1, :], in_=qn_w.rearrange("(o d) -> o d", o=1))
+        nc.gpsimd.dma_start(out=vectors[NORMED + 1 : NORMED + 2, :], in_=kn_w.rearrange("(o d) -> o d", o=1))
+        make_identity(nc, ident_bf16[:])
+        nc.gpsimd.dma_start(out=trig[:, 1, :, :], in_=freqs_cos.rearrange("(u p) j -> p u j", p=P))
+        nc.gpsimd.dma_start(out=trig[:, 2, :, :], in_=freqs_sin.rearrange("(u p) j -> p u j", p=P))
+        zero_plane(plane_rest)
+        zero_plane(plane_k)
+        zero_plane(plane_v)
+
+        everything = slice(0, PASSES)
+        load_x(0, 0)
+        load_x(0, 1)
+        load_scales(plane_first, Wq_scales[:, :, 0:BLOCK])
+        load_words(0, q_words(0), slice(0, 2))
+        load_x(1, 0)
+        load_x(1, 1)
+        load_x(2, 0)
+        load_x(2, 1)
+        load_words(0, q_words(0), slice(2, 4))
+        load_x(3, 0)
+        load_x(3, 1)
+        load_scales(plane_rest, Wq_scales[:, :, BLOCK : 4 * BLOCK])
+        load_words(1, q_words(1), everything)
+        load_words(2, q_words(2), everything)
+        load_scales(plane_k, Wk_scales)
+        load_scales(plane_v, Wv_scales)
+        load_words(3, q_words(3), everything)
+        load_words(4, Wk_words, everything)
+        load_words(5, Wv_words, everything)
+        nc.sync.dma_start(out=bv_rows[:], in_=bv.partition_broadcast(P))
+
+        def turn_x(g):
+            banks = []
+            for a in range(2):
+                bank = psum.tile([P, 2, 2, P], F32, name="xt", tag="turn%d" % ((2 * g + a) % BANKS))
+                pairs = x_sb[g][a][:].rearrange("p i k -> p (i k)").bitcast(F32)
+                for i in range(2):
+                    for u in range(2):
+                        nc.tensor.transpose(bank[:, i, u, :], pairs[:, 256 * i + u : 256 * (i + 1) : 2], ident_f32[:])
+                banks.append(bank)
+            return banks
+
+        def quantize_x(g, banks):
+            halves = []
+            for a in range(2):
+                half = x_grouped[g][:, 256 * a : 256 * (a + 1), :].rearrange("p r t -> p (r t)")
+                halves.append(half)
+                dst = half.bitcast(F32).rearrange("p (i r u) -> p i r u", i=2, u=2)
+                src = banks[a][:].rearrange("p i u r -> p i r u")
+                if a == 0:
+                    nc.vector.tensor_copy(out=dst, in_=src)
+                else:
+                    nc.scalar.copy(out=dst, in_=src)
+            for a in range(2):
+                cols = slice(256 * a, 256 * (a + 1))
+                nc.vector.quantize_mx(out=x_codes[g][:, cols].bitcast(E5M2X4), scales=x_scales[g][:, cols], in_=halves[a])
+
+        def head_plane(h, g):
+            j, c = divmod(h, HEADS_PER_BLOCK)
+            if j == 0:
+                return plane_first[:, g, D * c : D * (c + 1)]
+            if j == 4:
+                return plane_k[:, g, D * c : D * (c + 1)]
+            return plane_rest[:, g, D * (h - HEADS_PER_BLOCK) : D * (h - HEADS_PER_BLOCK + 1)]
+
+        sums = {}
+        biased = {}
+        turned = {}
+        roots = {}
+        inverse = {}
+        staged = {}
+
+        def project_pass(h, g):
+            if g == 0:
+                sums[h] = psum.tile([P, TOKENS], F32, name="sums", tag="sum%d" % (h % BANKS))
+            j, c = divmod(h, HEADS_PER_BLOCK)
+            nc.tensor.matmul_mx(
+                out=sums[h][:],
+                lhsT=words[j][:, g, 2 * D * c : 2 * D * (c + 1)].bitcast(E2M1X4),
+                lhsT_scale=head_plane(h, g),
+                rhs=x_codes[g][:].bitcast(E5M2X4),
+                rhs_scale=x_scales[g][:],
+                start=(g == 0),
+                stop=(g == PASSES - 1),
+            )
+
+        def add_bias(h):
+            biased[h] = work.tile([P, TOKENS], F32, name="biased")
+            nc.scalar.activation(out=biased[h][:], in_=sums[h][:], func=ACT.Identity, bias=bias_cols[:, h : h + 1])
+
+        def project(h):
+            for g in range(PASSES):
+                project_pass(h, g)
+            add_bias(h)
+
+        def turn_head(h):
+            turned[h] = psum.tile([P, TILES, D], F32, name="turned", tag="turn%d" % (h % BANKS))
+            for i in range(TILES):
+                nc.tensor.transpose(turned[h][:, i, :], biased[h][:, P * i : P * (i + 1)], ident_f32[:])
+
+        def root_mean_square(h):
+            squares = work.tile([P, TILES], F32, name="squares")
+            for i in range(TILES):
+                unread = work.tile([P, D], BF16, name="unread")
+                nc.scalar.activation(out=unread[:], in_=turned[h][:, i, :], func=ACT.Square, accum_out=squares[:, i : i + 1])
+            roots[h] = work.tile([P, TILES], F32, name="roots")
+            nc.scalar.activation(out=roots[h][:], in_=squares[:], func=ACT.Sqrt, scale=1.0 / D, bias=EPS)
+
+        def invert(h):
+            inverse[h] = work.tile([P, TILES], F32, name="inverse")
+            nc.vector.reciprocal(out=inverse[h][:], in_=roots[h][:])
+
+        def rotate(h, invert_next):
+            table = tables[0 if h < H else 1]
+            terms = [work.tile([P, TILES, D // 2, 2], F32, name="term%d" % e) for e in range(2)]
+            for i in range(TILES):
+                if invert_next and i == TILES - 1:
+                    invert(h + 1)
+                pairs = turned[h][:, i, :].rearrange("p (j e) -> p j e", e=2)
+                for e in range(2):
+                    nc.vector.scalar_tensor_tensor(
+                        out=terms[e][:, i, :, :],
+                        in0=pairs[:, :, e : e + 1].to_broadcast([P, D // 2, 2]),
+                        scalar=inverse[h][:, i : i + 1],
+                        in1=table[e][:, i % 2, :, :],
+                        op0=ALU.mult,
+                        op1=ALU.mult,
+                    )
+            if h % 2 == 0:
+                staged[h // 2] = work.tile([P, TILES, 2 * D], F32, name="staged")
+            nc.gpsimd.tensor_tensor(
+                out=staged[h // 2][:, :, D * (h % 2) : D * (h % 2 + 1)],
+                in0=terms[0][:].rearrange("p i j e -> p i (j e)"),
+                in1=terms[1][:].rearrange("p i j e -> p i (j e)"),
+                op=ALU.add,
+            )
+
+        def store_heads(first, count):
+            rows, col = (q_rows, D * first) if first < H else (k_rows, D * (first - H))
+            off = D * (first % 2)
+            nc.sync.dma_start(out=rows[:, :, col : col + D * count], in_=staged[first // 2][:, :, off : off + D * count])
+
+        def finish_pair(h):
+            root_mean_square(h)
+            root_mean_square(h + 1)
+            invert(h)
+            rotate(h, True)
+            if h + 2 == NORMED:
+                store_heads(h, 1)
+            rotate(h + 1, False)
+            if h + 2 == NORMED:
+                store_heads(h + 1, 1)
+            else:
+                store_heads(h, 2)
+
+        def project_v(i):
+            acc = psum.tile([P, BLOCK], F32, name="acc_v", tag="sum%d" % ((NORMED + i) % BANKS))
+            for g in range(PASSES):
+                nc.tensor.matmul_mx(
+                    out=acc[:],
+                    lhsT=x_codes[g][:, P * i : P * (i + 1)].bitcast(E5M2X4),
+                    lhsT_scale=x_scales[g][:, P * i : P * (i + 1)],
+                    rhs=words[5][:, g, :].bitcast(E2M1X4),
+                    rhs_scale=plane_v[:, g, :],
+                    start=(g == 0),
+                    stop=(g == PASSES - 1),
+                )
+            return acc
+
+        def finish_v(i, acc):
+            result = work.tile([P, BLOCK], F32, name="result_v")
+            nc.vector.tensor_tensor(out=result[:], in0=acc[:], in1=bv_rows[:], op=ALU.add)
+            nc.sync.dma_start(out=v_rows[:, i, :], in_=result[:])
+
+        def spread_vectors():
+            bank = psum.tile([P, 2 * D + 32], F32, name="spread", tag="sum%d" % OPEN_AT_START)
+            nc.tensor.matmul(bank[:, 2 * D : 2 * D + 32], lhsT=vectors[:], rhs=ident_bf16[:, 0:32], start=True, stop=True)
+            for n in range(2):
+                row = NORMED + n
+                nc.tensor.matmul(
+                    bank[:, D * n : D * (n + 1)], lhsT=ident_bf16[:, row : row + 1].to_broadcast([P, P]),
+                    rhs=vectors[:], start=True, stop=True,
+                )
+            return bank
+
+        def build_tables(bank):
+            nc.scalar.copy(out=bias_cols[:], in_=bank[:, 2 * D : 2 * D + NORMED])
+            nc.vector.tensor_scalar(out=trig[:, 0, :, :], in0=trig[:, 2, :, :], scalar1=-1.0, scalar2=None, op0=ALU.mult)
+            for n in range(2):
+                gain = bank[:, D * n : D * (n + 1)].rearrange("p (o j e) -> p o j e", o=1, e=2)
+                for e in range(2):
+                    nc.vector.tensor_tensor(
+                        out=tables[n][e][:],
+                        in0=trig[:, 1 - e : 3 - e, :, :].rearrange("p s u j -> p u j s"),
+                        in1=gain[:, :, :, e : e + 1].to_broadcast([P, 2, D // 2, 2]),
+                        op=ALU.mult,
+                    )
+
+        quantize_x(0, turn_x(0))
+        for g in range(PASSES):
+            if g + 1 < PASSES:
+                quantize_x(g + 1, turn_x(g + 1))
+            if g + 2 == PASSES:
+                build_tables(spread_vectors())
+            for h in range(OPEN_AT_START):
+                project_pass(h, g)
+        for h in range(OPEN_AT_START):
+            add_bias(h)
+
+        project(3)
+        turn_head(0)
+        turn_head(1)
+        finish_pair(0)
+        project(4)
+        for h in range(2, NORMED - 2, 2):
+            turn_head(h)
+            turn_head(h + 1)
+            finish_pair(h)
+            for n in (h + 3, h + 4):
+                if n < NORMED:
+                    project(n)
+        acc_first = project_v(0)
+        turn_head(NORMED - 2)
+        turn_head(NORMED - 1)
+        finish_v(0, acc_first)
+        finish_pair(NORMED - 2)
+        for i in range(1, TILES):
+            finish_v(i, project_v(i))

@@ -25,8 +25,9 @@ PASSES = C // K_PASS
 NORMED = H + KV
 BLOCK = 512
 HEADS_PER_BLOCK = BLOCK // D
-OPEN_AT_START = 3
+OPEN_AT_START = 2
 BANKS = 4
+WORD_LOADS = [(0, 2), (2, 2), (4, 4), (8, 4), (12, 4), (16, 4), (20, 4)]
 
 
 def tile_llamacausalselfattention_pa_kernel(
@@ -48,25 +49,30 @@ def tile_llamacausalselfattention_pa_kernel(
         ident_f32 = keep.tile([P, P], F32, name="ident_f32")
         ident_bf16 = keep.tile([P, P], BF16, name="ident_bf16")
         vectors = keep.tile([P, D], BF16, name="vectors")
-        trig = keep.tile([P, 3, 2, D // 2], BF16, name="trig")
-        bias_cols = keep.tile([P, NORMED], F32, name="bias_cols")
+        trig = keep.tile([P, 4, 2, D // 2], BF16, name="trig")
+        spread = keep.tile([P, 2 * D + NORMED], F32, name="spread")
         bv_rows = keep.tile([P, BLOCK], BF16, name="bv_rows")
-        x_sb = [[keep.tile([P, 2, K_PASS], BF16, name="x_%d_%d" % (g, a)) for a in range(2)] for g in range(PASSES)]
+        x_sb = [keep.tile([P, TILES, K_PASS], BF16, name="x_%d" % g) for g in range(PASSES)]
         x_grouped = [keep.tile([P, TOKENS, 4], BF16, name="xg_%d" % g, align_bytes=64) for g in range(PASSES)]
         x_codes = [keep.tile([P, TOKENS], U32, name="xc_%d" % g, align_bytes=64) for g in range(PASSES)]
         x_scales = [keep.tile([P, TOKENS], U8, name="xs_%d" % g, align_bytes=64) for g in range(PASSES)]
-        words = [keep.tile([P, PASSES, 2 * BLOCK], U8, name="words_%d" % j, align_bytes=64) for j in range(6)]
+        words = {
+            first: keep.tile([P, PASSES, 2 * D * count], U8, name="words_%d" % first, align_bytes=64)
+            for first, count in WORD_LOADS
+        }
         plane_first = keep.tile([P, PASSES, BLOCK], U8, name="plane_first", align_bytes=64)
         plane_rest = keep.tile([P, PASSES, 3 * BLOCK], U8, name="plane_rest", align_bytes=64)
         plane_k = keep.tile([P, PASSES, BLOCK], U8, name="plane_k", align_bytes=64)
         plane_v = keep.tile([P, PASSES, BLOCK], U8, name="plane_v", align_bytes=64)
-        tables = [[keep.tile([P, 2, D // 2, 2], F32, name="table_%d_%d" % (n, e)) for e in range(2)] for n in range(2)]
+        tables = [keep.tile([P, 2, D, 2], F32, name="table_%d" % n) for n in range(2)]
 
         def zero_plane(plane):
             nc.vector.memset(plane[:].rearrange("p g n -> p (g n)").bitcast(I32), 0)
 
-        def load_x(g, a):
-            nc.sync.dma_start(out=x_sb[g][a][:], in_=x_rows[:, 2 * a : 2 * a + 2, K_PASS * g : K_PASS * (g + 1)])
+        def load_x(g):
+            for a in range(2):
+                tiles = slice(2 * a, 2 * a + 2)
+                nc.sync.dma_start(out=x_sb[g][:, tiles, :], in_=x_rows[:, tiles, K_PASS * g : K_PASS * (g + 1)])
 
         def load_scales(plane, scales):
             for q in range(4):
@@ -75,56 +81,47 @@ def tile_llamacausalselfattention_pa_kernel(
                     in_=scales[:, 4 * q : 4 * q + 4, :].rearrange("g r n -> r g n").bitcast(I32),
                 )
 
-        def load_words(j, src, passes):
-            nc.sync.dma_start(
-                out=words[j][:, passes, :].bitcast(I32),
-                in_=src[passes, :, :].rearrange("g p n -> p g n").bitcast(I32),
-            )
+        def load_words(first, src):
+            nc.sync.dma_start(out=words[first][:].bitcast(I32), in_=src.rearrange("g p n -> p g n").bitcast(I32))
 
-        def q_words(j):
-            return Wq_words[:, :, 2 * BLOCK * j : 2 * BLOCK * (j + 1)]
+        def load_q_words(first, count):
+            load_words(first, Wq_words[:, :, 2 * D * first : 2 * D * (first + count)])
 
         zero_plane(plane_first)
-        nc.vector.memset(vectors[:], 0.0)
         make_identity(nc, ident_f32[:])
+        nc.gpsimd.memset(vectors[:], 0.0)
         nc.gpsimd.dma_start(out=vectors[0:H, :], in_=bq.rearrange("(h d) -> h d", d=D))
         nc.gpsimd.dma_start(out=vectors[H:NORMED, :], in_=bk.rearrange("(h d) -> h d", d=D))
         nc.gpsimd.dma_start(out=vectors[NORMED : NORMED + 1, :], in_=qn_w.rearrange("(o d) -> o d", o=1))
         nc.gpsimd.dma_start(out=vectors[NORMED + 1 : NORMED + 2, :], in_=kn_w.rearrange("(o d) -> o d", o=1))
-        make_identity(nc, ident_bf16[:])
-        nc.gpsimd.dma_start(out=trig[:, 1, :, :], in_=freqs_cos.rearrange("(u p) j -> p u j", p=P))
-        nc.gpsimd.dma_start(out=trig[:, 2, :, :], in_=freqs_sin.rearrange("(u p) j -> p u j", p=P))
+        nc.gpsimd.dma_start(out=trig[:, 0, :, :], in_=freqs_cos.rearrange("(u p) j -> p u j", p=P))
+        nc.gpsimd.dma_start(out=trig[:, 1, :, :], in_=freqs_sin.rearrange("(u p) j -> p u j", p=P))
         zero_plane(plane_rest)
         zero_plane(plane_k)
         zero_plane(plane_v)
+        nc.vector.tensor_copy(out=ident_bf16[:], in_=ident_f32[:])
 
-        everything = slice(0, PASSES)
-        load_x(0, 0)
-        load_x(0, 1)
+        load_x(0)
         load_scales(plane_first, Wq_scales[:, :, 0:BLOCK])
-        load_words(0, q_words(0), slice(0, 2))
-        load_x(1, 0)
-        load_x(1, 1)
-        load_x(2, 0)
-        load_x(2, 1)
-        load_words(0, q_words(0), slice(2, 4))
-        load_x(3, 0)
-        load_x(3, 1)
+        load_q_words(0, 2)
+        for g in range(1, PASSES):
+            load_x(g)
+        load_q_words(2, 2)
         load_scales(plane_rest, Wq_scales[:, :, BLOCK : 4 * BLOCK])
-        load_words(1, q_words(1), everything)
-        load_words(2, q_words(2), everything)
+        load_q_words(4, 4)
+        load_q_words(8, 4)
         load_scales(plane_k, Wk_scales)
         load_scales(plane_v, Wv_scales)
-        load_words(3, q_words(3), everything)
-        load_words(4, Wk_words, everything)
-        load_words(5, Wv_words, everything)
+        load_q_words(12, 4)
+        load_words(H, Wk_words)
+        load_words(NORMED, Wv_words)
         nc.sync.dma_start(out=bv_rows[:], in_=bv.partition_broadcast(P))
 
         def turn_x(g):
             banks = []
             for a in range(2):
                 bank = psum.tile([P, 2, 2, P], F32, name="xt", tag="turn%d" % ((2 * g + a) % BANKS))
-                pairs = x_sb[g][a][:].rearrange("p i k -> p (i k)").bitcast(F32)
+                pairs = x_sb[g][:, 2 * a : 2 * a + 2, :].rearrange("p i k -> p (i k)").bitcast(F32)
                 for i in range(2):
                     for u in range(2):
                         nc.tensor.transpose(bank[:, i, u, :], pairs[:, 256 * i + u : 256 * (i + 1) : 2], ident_f32[:])
@@ -157,17 +154,16 @@ def tile_llamacausalselfattention_pa_kernel(
         sums = {}
         biased = {}
         turned = {}
-        roots = {}
         inverse = {}
-        staged = {}
 
         def project_pass(h, g):
             if g == 0:
                 sums[h] = psum.tile([P, TOKENS], F32, name="sums", tag="sum%d" % (h % BANKS))
-            j, c = divmod(h, HEADS_PER_BLOCK)
+            first = max(f for f, count in WORD_LOADS if f <= h)
+            c = h - first
             nc.tensor.matmul_mx(
                 out=sums[h][:],
-                lhsT=words[j][:, g, 2 * D * c : 2 * D * (c + 1)].bitcast(E2M1X4),
+                lhsT=words[first][:, g, 2 * D * c : 2 * D * (c + 1)].bitcast(E2M1X4),
                 lhsT_scale=head_plane(h, g),
                 rhs=x_codes[g][:].bitcast(E5M2X4),
                 rhs_scale=x_scales[g][:],
@@ -177,7 +173,11 @@ def tile_llamacausalselfattention_pa_kernel(
 
         def add_bias(h):
             biased[h] = work.tile([P, TOKENS], F32, name="biased")
-            nc.scalar.activation(out=biased[h][:], in_=sums[h][:], func=ACT.Identity, bias=bias_cols[:, h : h + 1])
+            bias = spread[:, 2 * D + h : 2 * D + h + 1]
+            if h % 4 == 0 and h > 0:
+                nc.vector.tensor_scalar(out=biased[h][:], in0=sums[h][:], scalar1=bias, scalar2=None, op0=ALU.add)
+            else:
+                nc.scalar.activation(out=biased[h][:], in_=sums[h][:], func=ACT.Identity, bias=bias)
 
         def project(h):
             for g in range(PASSES):
@@ -194,55 +194,37 @@ def tile_llamacausalselfattention_pa_kernel(
             for i in range(TILES):
                 unread = work.tile([P, D], BF16, name="unread")
                 nc.scalar.activation(out=unread[:], in_=turned[h][:, i, :], func=ACT.Square, accum_out=squares[:, i : i + 1])
-            roots[h] = work.tile([P, TILES], F32, name="roots")
-            nc.scalar.activation(out=roots[h][:], in_=squares[:], func=ACT.Sqrt, scale=1.0 / D, bias=EPS)
-
-        def invert(h):
             inverse[h] = work.tile([P, TILES], F32, name="inverse")
-            nc.vector.reciprocal(out=inverse[h][:], in_=roots[h][:])
+            nc.scalar.activation(out=inverse[h][:], in_=squares[:], func=ACT.Abs_reciprocal_sqrt, scale=1.0 / D, bias=EPS)
 
-        def rotate(h, invert_next):
+        def rotate(h):
             table = tables[0 if h < H else 1]
-            terms = [work.tile([P, TILES, D // 2, 2], F32, name="term%d" % e) for e in range(2)]
+            terms = work.tile([P, TILES, D, 2], F32, name="terms")
             for i in range(TILES):
-                if invert_next and i == TILES - 1:
-                    invert(h + 1)
-                pairs = turned[h][:, i, :].rearrange("p (j e) -> p j e", e=2)
-                for e in range(2):
-                    nc.vector.scalar_tensor_tensor(
-                        out=terms[e][:, i, :, :],
-                        in0=pairs[:, :, e : e + 1].to_broadcast([P, D // 2, 2]),
-                        scalar=inverse[h][:, i : i + 1],
-                        in1=table[e][:, i % 2, :, :],
-                        op0=ALU.mult,
-                        op1=ALU.mult,
-                    )
-            if h % 2 == 0:
-                staged[h // 2] = work.tile([P, TILES, 2 * D], F32, name="staged")
+                nc.vector.scalar_tensor_tensor(
+                    out=terms[:, i, :, :],
+                    in0=table[:, i % 2, :, :],
+                    scalar=inverse[h][:, i : i + 1],
+                    in1=turned[h][:, i, :].unsqueeze(2).to_broadcast([P, D, 2]),
+                    op0=ALU.mult,
+                    op1=ALU.mult,
+                )
+            rotated = work.tile([P, TILES, D], F32, name="rotated")
+            by_pair = terms[:].rearrange("p i (j e) c -> p (i j) e c", e=2)
             nc.gpsimd.tensor_tensor(
-                out=staged[h // 2][:, :, D * (h % 2) : D * (h % 2 + 1)],
-                in0=terms[0][:].rearrange("p i j e -> p i (j e)"),
-                in1=terms[1][:].rearrange("p i j e -> p i (j e)"),
+                out=rotated[:].rearrange("p i (j c) -> p (i j) c", c=2),
+                in0=by_pair[:, :, 0, :],
+                in1=by_pair[:, :, 1, :],
                 op=ALU.add,
             )
-
-        def store_heads(first, count):
-            rows, col = (q_rows, D * first) if first < H else (k_rows, D * (first - H))
-            off = D * (first % 2)
-            nc.sync.dma_start(out=rows[:, :, col : col + D * count], in_=staged[first // 2][:, :, off : off + D * count])
+            rows, col = (q_rows, D * h) if h < H else (k_rows, D * (h - H))
+            nc.sync.dma_start(out=rows[:, :, col : col + D], in_=rotated[:])
 
         def finish_pair(h):
             root_mean_square(h)
             root_mean_square(h + 1)
-            invert(h)
-            rotate(h, True)
-            if h + 2 == NORMED:
-                store_heads(h, 1)
-            rotate(h + 1, False)
-            if h + 2 == NORMED:
-                store_heads(h + 1, 1)
-            else:
-                store_heads(h, 2)
+            rotate(h)
+            rotate(h + 1)
 
         def project_v(i):
             acc = psum.tile([P, BLOCK], F32, name="acc_v", tag="sum%d" % ((NORMED + i) % BANKS))
@@ -251,7 +233,7 @@ def tile_llamacausalselfattention_pa_kernel(
                     out=acc[:],
                     lhsT=x_codes[g][:, P * i : P * (i + 1)].bitcast(E5M2X4),
                     lhsT_scale=x_scales[g][:, P * i : P * (i + 1)],
-                    rhs=words[5][:, g, :].bitcast(E2M1X4),
+                    rhs=words[NORMED][:, g, :].bitcast(E2M1X4),
                     rhs_scale=plane_v[:, g, :],
                     start=(g == 0),
                     stop=(g == PASSES - 1),
@@ -260,11 +242,11 @@ def tile_llamacausalselfattention_pa_kernel(
 
         def finish_v(i, acc):
             result = work.tile([P, BLOCK], F32, name="result_v")
-            nc.vector.tensor_tensor(out=result[:], in0=acc[:], in1=bv_rows[:], op=ALU.add)
+            nc.vector.tensor_tensor(out=result[:], in0=bv_rows[:], in1=acc[:], op=ALU.add)
             nc.sync.dma_start(out=v_rows[:, i, :], in_=result[:])
 
         def spread_vectors():
-            bank = psum.tile([P, 2 * D + 32], F32, name="spread", tag="sum%d" % OPEN_AT_START)
+            bank = psum.tile([P, 2 * D + 32], F32, name="spread_bank", tag="sum%d" % (BANKS - 1))
             nc.tensor.matmul(bank[:, 2 * D : 2 * D + 32], lhsT=vectors[:], rhs=ident_bf16[:, 0:32], start=True, stop=True)
             for n in range(2):
                 row = NORMED + n
@@ -272,41 +254,39 @@ def tile_llamacausalselfattention_pa_kernel(
                     bank[:, D * n : D * (n + 1)], lhsT=ident_bf16[:, row : row + 1].to_broadcast([P, P]),
                     rhs=vectors[:], start=True, stop=True,
                 )
-            return bank
+            nc.scalar.copy(out=spread[:], in_=bank[:, 0 : 2 * D + NORMED])
 
-        def build_tables(bank):
-            nc.scalar.copy(out=bias_cols[:], in_=bank[:, 2 * D : 2 * D + NORMED])
-            nc.vector.tensor_scalar(out=trig[:, 0, :, :], in0=trig[:, 2, :, :], scalar1=-1.0, scalar2=None, op0=ALU.mult)
-            for n in range(2):
-                gain = bank[:, D * n : D * (n + 1)].rearrange("p (o j e) -> p o j e", o=1, e=2)
-                for e in range(2):
-                    nc.vector.tensor_tensor(
-                        out=tables[n][e][:],
-                        in0=trig[:, 1 - e : 3 - e, :, :].rearrange("p s u j -> p u j s"),
-                        in1=gain[:, :, :, e : e + 1].to_broadcast([P, 2, D // 2, 2]),
-                        op=ALU.mult,
-                    )
+        def build_table(engine, n):
+            gain = spread[:, D * n : D * (n + 1)].rearrange("p (j e o) -> p j e o", e=2, o=1)
+            for u in range(2):
+                engine.tensor_tensor(
+                    out=tables[n][:, u, :, :].rearrange("p (j e) c -> p j e c", e=2),
+                    in0=trig[:, :, u, :].rearrange("p (e c) j -> p j e c", e=2),
+                    in1=gain.to_broadcast([P, D // 2, 2, 2]),
+                    op=ALU.mult,
+                )
 
         quantize_x(0, turn_x(0))
         for g in range(PASSES):
             if g + 1 < PASSES:
                 quantize_x(g + 1, turn_x(g + 1))
             if g + 2 == PASSES:
-                build_tables(spread_vectors())
+                spread_vectors()
+                nc.vector.tensor_scalar(out=trig[:, 2, :, :], in0=trig[:, 1, :, :], scalar1=-1.0, scalar2=None, op0=ALU.mult)
+                nc.vector.tensor_copy(out=trig[:, 3, :, :], in_=trig[:, 0, :, :])
+                build_table(nc.vector, 0)
             for h in range(OPEN_AT_START):
                 project_pass(h, g)
         for h in range(OPEN_AT_START):
             add_bias(h)
 
-        project(3)
-        turn_head(0)
-        turn_head(1)
-        finish_pair(0)
-        project(4)
-        for h in range(2, NORMED - 2, 2):
+        project(OPEN_AT_START)
+        for h in range(0, NORMED - 2, 2):
             turn_head(h)
             turn_head(h + 1)
             finish_pair(h)
+            if h == 0:
+                build_table(nc.gpsimd, 1)
             for n in (h + 3, h + 4):
                 if n < NORMED:
                     project(n)

@@ -67,7 +67,10 @@ def tile_llamacausalselfattention_pa_kernel(
         tables = [keep.tile([P, 2, D, 2], F32, name="table_%d" % n) for n in range(2)]
 
         def zero_plane(plane):
-            nc.vector.memset(plane[:].rearrange("p g n -> p (g n)").bitcast(I32), 0)
+            filler = plane[:].rearrange("p g n -> p (g n)").bitcast(I32)
+            cut = filler.shape[1] // 2 + 1
+            nc.vector.memset(filler[:, 0:cut], 0)
+            nc.vector.memset(filler[:, cut:], 0)
 
         def load_x(g):
             for a in range(2):
@@ -97,8 +100,6 @@ def tile_llamacausalselfattention_pa_kernel(
         nc.gpsimd.dma_start(out=trig[:, 0, :, :], in_=freqs_cos.rearrange("(u p) j -> p u j", p=P))
         nc.gpsimd.dma_start(out=trig[:, 1, :, :], in_=freqs_sin.rearrange("(u p) j -> p u j", p=P))
         zero_plane(plane_rest)
-        zero_plane(plane_k)
-        zero_plane(plane_v)
         nc.vector.tensor_copy(out=ident_bf16[:], in_=ident_f32[:])
 
         load_x(0)
@@ -110,12 +111,6 @@ def tile_llamacausalselfattention_pa_kernel(
         load_scales(plane_rest, Wq_scales[:, :, BLOCK : 4 * BLOCK])
         load_q_words(4, 4)
         load_q_words(8, 4)
-        load_scales(plane_k, Wk_scales)
-        load_scales(plane_v, Wv_scales)
-        load_q_words(12, 4)
-        load_words(H, Wk_words)
-        load_words(NORMED, Wv_words)
-        nc.sync.dma_start(out=bv_rows[:], in_=bv.partition_broadcast(P))
 
         def turn_x(g):
             banks = []
@@ -154,6 +149,7 @@ def tile_llamacausalselfattention_pa_kernel(
         sums = {}
         biased = {}
         turned = {}
+        squares = {}
         inverse = {}
 
         def project_pass(h, g):
@@ -174,7 +170,7 @@ def tile_llamacausalselfattention_pa_kernel(
         def add_bias(h):
             biased[h] = work.tile([P, TOKENS], F32, name="biased")
             bias = spread[:, 2 * D + h : 2 * D + h + 1]
-            if h % 4 == 0 and h > 0:
+            if h % 2 == 0 and OPEN_AT_START < h < H:
                 nc.vector.tensor_scalar(out=biased[h][:], in0=sums[h][:], scalar1=bias, scalar2=None, op0=ALU.add)
             else:
                 nc.scalar.activation(out=biased[h][:], in_=sums[h][:], func=ACT.Identity, bias=bias)
@@ -189,13 +185,16 @@ def tile_llamacausalselfattention_pa_kernel(
             for i in range(TILES):
                 nc.tensor.transpose(turned[h][:, i, :], biased[h][:, P * i : P * (i + 1)], ident_f32[:])
 
-        def root_mean_square(h):
-            squares = work.tile([P, TILES], F32, name="squares")
-            for i in range(TILES):
+        def sum_squares(h, tiles):
+            if h not in squares:
+                squares[h] = work.tile([P, TILES], F32, name="squares")
+            for i in tiles:
                 unread = work.tile([P, D], BF16, name="unread")
-                nc.scalar.activation(out=unread[:], in_=turned[h][:, i, :], func=ACT.Square, accum_out=squares[:, i : i + 1])
+                nc.scalar.activation(out=unread[:], in_=turned[h][:, i, :], func=ACT.Square, accum_out=squares[h][:, i : i + 1])
+
+        def invert(h):
             inverse[h] = work.tile([P, TILES], F32, name="inverse")
-            nc.scalar.activation(out=inverse[h][:], in_=squares[:], func=ACT.Abs_reciprocal_sqrt, scale=1.0 / D, bias=EPS)
+            nc.scalar.activation(out=inverse[h][:], in_=squares[h][:], func=ACT.Abs_reciprocal_sqrt, scale=1.0 / D, bias=EPS)
 
         def rotate(h):
             table = tables[0 if h < H else 1]
@@ -209,7 +208,7 @@ def tile_llamacausalselfattention_pa_kernel(
                     op0=ALU.mult,
                     op1=ALU.mult,
                 )
-            rotated = work.tile([P, TILES, D], F32, name="rotated")
+            rotated = work.tile([P, TILES, D], F32, name="rotated", bufs=8)
             by_pair = terms[:].rearrange("p i (j e) c -> p (i j) e c", e=2)
             nc.gpsimd.tensor_tensor(
                 out=rotated[:].rearrange("p i (j c) -> p (i j) c", c=2),
@@ -219,12 +218,6 @@ def tile_llamacausalselfattention_pa_kernel(
             )
             rows, col = (q_rows, D * h) if h < H else (k_rows, D * (h - H))
             nc.sync.dma_start(out=rows[:, :, col : col + D], in_=rotated[:])
-
-        def finish_pair(h):
-            root_mean_square(h)
-            root_mean_square(h + 1)
-            rotate(h)
-            rotate(h + 1)
 
         def project_v(i):
             acc = psum.tile([P, BLOCK], F32, name="acc_v", tag="sum%d" % ((NORMED + i) % BANKS))
@@ -270,30 +263,43 @@ def tile_llamacausalselfattention_pa_kernel(
         for g in range(PASSES):
             if g + 1 < PASSES:
                 quantize_x(g + 1, turn_x(g + 1))
+            for h in range(OPEN_AT_START):
+                project_pass(h, g)
             if g + 2 == PASSES:
                 spread_vectors()
                 nc.vector.tensor_scalar(out=trig[:, 2, :, :], in0=trig[:, 1, :, :], scalar1=-1.0, scalar2=None, op0=ALU.mult)
                 nc.vector.tensor_copy(out=trig[:, 3, :, :], in_=trig[:, 0, :, :])
                 build_table(nc.vector, 0)
-            for h in range(OPEN_AT_START):
-                project_pass(h, g)
+        zero_plane(plane_k)
+        zero_plane(plane_v)
+        load_scales(plane_k, Wk_scales)
+        load_scales(plane_v, Wv_scales)
+        load_q_words(12, 4)
+        load_words(H, Wk_words)
+        load_words(NORMED, Wv_words)
         for h in range(OPEN_AT_START):
             add_bias(h)
 
         project(OPEN_AT_START)
-        for h in range(0, NORMED - 2, 2):
+        for h in range(0, NORMED, 2):
             turn_head(h)
             turn_head(h + 1)
-            finish_pair(h)
+            sum_squares(h, range(TILES))
+            sum_squares(h + 1, range(1))
+            invert(h)
+            sum_squares(h + 1, range(1, TILES))
+            if h + 3 < NORMED:
+                project(h + 3)
+            invert(h + 1)
+            rotate(h)
+            rotate(h + 1)
             if h == 0:
                 build_table(nc.gpsimd, 1)
-            for n in (h + 3, h + 4):
-                if n < NORMED:
-                    project(n)
-        acc_first = project_v(0)
-        turn_head(NORMED - 2)
-        turn_head(NORMED - 1)
-        finish_v(0, acc_first)
-        finish_pair(NORMED - 2)
+            if h == H // 2:
+                nc.sync.dma_start(out=bv_rows[:], in_=bv.partition_broadcast(P))
+            if h + 4 < NORMED:
+                project(h + 4)
+            if h + 4 == NORMED:
+                finish_v(0, project_v(0))
         for i in range(1, TILES):
             finish_v(i, project_v(i))

@@ -92,6 +92,8 @@ def tile_llamacausalselfattention_pa_kernel(
 
         zero_plane(plane_first)
         make_identity(nc, ident_f32[:])
+        table_preload = keep.tile([P, 1], F32, name="table_preload")
+        nc.scalar.activation(out=table_preload[:], in_=ident_f32[:, 0:1], func=ACT.Abs_reciprocal_sqrt, bias=1.0)
         nc.gpsimd.memset(vectors[:], 0.0)
         nc.gpsimd.dma_start(out=vectors[0:H, :], in_=bq.rearrange("(h d) -> h d", d=D))
         nc.gpsimd.dma_start(out=vectors[H:NORMED, :], in_=bk.rearrange("(h d) -> h d", d=D))
@@ -104,8 +106,9 @@ def tile_llamacausalselfattention_pa_kernel(
 
         load_x(0)
         load_scales(plane_first, Wq_scales[:, :, 0:BLOCK])
+        load_x(1)
         load_q_words(0, 2)
-        for g in range(1, PASSES):
+        for g in range(2, PASSES):
             load_x(g)
         load_q_words(2, 2)
         load_scales(plane_rest, Wq_scales[:, :, BLOCK : 4 * BLOCK])
@@ -196,28 +199,42 @@ def tile_llamacausalselfattention_pa_kernel(
             inverse[h] = work.tile([P, TILES], F32, name="inverse")
             nc.scalar.activation(out=inverse[h][:], in_=squares[h][:], func=ACT.Abs_reciprocal_sqrt, scale=1.0 / D, bias=EPS)
 
-        def rotate(h):
+        def multiply(h, terms):
             table = tables[0 if h < H else 1]
-            terms = work.tile([P, TILES, D, 2], F32, name="terms")
             for i in range(TILES):
                 nc.vector.scalar_tensor_tensor(
-                    out=terms[:, i, :, :],
+                    out=terms[:, i, h % 2, :, :],
                     in0=table[:, i % 2, :, :],
                     scalar=inverse[h][:, i : i + 1],
                     in1=turned[h][:, i, :].unsqueeze(2).to_broadcast([P, D, 2]),
                     op0=ALU.mult,
                     op1=ALU.mult,
                 )
-            rotated = work.tile([P, TILES, D], F32, name="rotated", bufs=8)
-            by_pair = terms[:].rearrange("p i (j e) c -> p (i j) e c", e=2)
+
+        def add_and_store(first, count, terms, rotated):
+            heads = slice(first % 2, first % 2 + count)
+            by_pair = terms[:, :, heads, :, :].rearrange("p i n (j e) c -> p i (n j) e c", e=2)
+            result = rotated[:, :, heads, :].rearrange("p i n d -> p i (n d)")
             nc.gpsimd.tensor_tensor(
-                out=rotated[:].rearrange("p i (j c) -> p (i j) c", c=2),
-                in0=by_pair[:, :, 0, :],
-                in1=by_pair[:, :, 1, :],
+                out=result.rearrange("p i (j c) -> p i j c", c=2),
+                in0=by_pair[:, :, :, 0, :],
+                in1=by_pair[:, :, :, 1, :],
                 op=ALU.add,
             )
-            rows, col = (q_rows, D * h) if h < H else (k_rows, D * (h - H))
-            nc.sync.dma_start(out=rows[:, :, col : col + D], in_=rotated[:])
+            rows, col = (q_rows, D * first) if first < H else (k_rows, D * (first - H))
+            nc.sync.dma_start(out=rows[:, :, col : col + D * count], in_=result)
+
+        def rotate_pair(h):
+            terms = work.tile([P, TILES, 2, D, 2], F32, name="terms", bufs=3)
+            rotated = work.tile([P, TILES, 2, D], F32, name="rotated")
+            if h < H:
+                multiply(h, terms)
+                multiply(h + 1, terms)
+                add_and_store(h, 2, terms, rotated)
+            else:
+                for n in (h, h + 1):
+                    multiply(n, terms)
+                    add_and_store(n, 1, terms, rotated)
 
         def project_v(i):
             acc = psum.tile([P, BLOCK], F32, name="acc_v", tag="sum%d" % ((NORMED + i) % BANKS))
@@ -249,10 +266,10 @@ def tile_llamacausalselfattention_pa_kernel(
                 )
             nc.scalar.copy(out=spread[:], in_=bank[:, 0 : 2 * D + NORMED])
 
-        def build_table(engine, n):
+        def build_table(n):
             gain = spread[:, D * n : D * (n + 1)].rearrange("p (j e o) -> p j e o", e=2, o=1)
             for u in range(2):
-                engine.tensor_tensor(
+                nc.vector.tensor_tensor(
                     out=tables[n][:, u, :, :].rearrange("p (j e) c -> p j e c", e=2),
                     in0=trig[:, :, u, :].rearrange("p (e c) j -> p j e c", e=2),
                     in1=gain.to_broadcast([P, D // 2, 2, 2]),
@@ -269,7 +286,8 @@ def tile_llamacausalselfattention_pa_kernel(
                 spread_vectors()
                 nc.vector.tensor_scalar(out=trig[:, 2, :, :], in0=trig[:, 1, :, :], scalar1=-1.0, scalar2=None, op0=ALU.mult)
                 nc.vector.tensor_copy(out=trig[:, 3, :, :], in_=trig[:, 0, :, :])
-                build_table(nc.vector, 0)
+                build_table(0)
+                build_table(1)
         zero_plane(plane_k)
         zero_plane(plane_v)
         load_scales(plane_k, Wk_scales)
@@ -291,10 +309,7 @@ def tile_llamacausalselfattention_pa_kernel(
             if h + 3 < NORMED:
                 project(h + 3)
             invert(h + 1)
-            rotate(h)
-            rotate(h + 1)
-            if h == 0:
-                build_table(nc.gpsimd, 1)
+            rotate_pair(h)
             if h == H // 2:
                 nc.sync.dma_start(out=bv_rows[:], in_=bv.partition_broadcast(P))
             if h + 4 < NORMED:

from contextlib import ExitStack

import concourse.mybir as mybir
from concourse.masks import make_identity

B, T, C, H, KV, D = 2, 256, 2048, 16, 4, 128
EPS = 1e-5
FLOPS = 2 * B * T * C * (H + 2 * KV) * D

F32 = mybir.dt.float32
BF16 = mybir.dt.bfloat16
I32 = mybir.dt.int32
U32 = mybir.dt.uint32
U8 = mybir.dt.uint8
E5M2X4 = mybir.dt.float8_e5m2_x4
E2M1X4 = mybir.dt.float4_e2m1fn_x4
ALU = mybir.AluOpType
ACT = mybir.ActivationFunctionType

P = 128
TOKENS = B * T
TILES = TOKENS // P
K_PASS = 512
PASSES = C // K_PASS
NORMED = H + KV
BLOCK = 512
HEADS_PER_BLOCK = BLOCK // D
OPEN_AT_START = 2
BANKS = 4
WORD_LOADS = [(0, 2), (2, 2), (4, 4), (8, 4), (12, 4), (16, 4), (20, 4)]


def tile_llamacausalselfattention_pa_kernel(
    tc, x, Wq_words, Wq_scales, bq, Wk_words, Wk_scales, bk, Wv_words, Wv_scales, bv,
    qn_w, kn_w, freqs_cos, freqs_sin, out_0, out_1, out_2,
):
    nc = tc.nc
    x_rows = x.rearrange("b (u p) c -> p (b u) c", p=P)
    q_rows = out_0.rearrange("b (u p) h d -> p (b u) (h d)", p=P)
    k_rows = out_1.rearrange("b (u p) h d -> p (b u) (h d)", p=P)
    v_rows = out_2.rearrange("b (u p) h d -> p (b u) (h d)", p=P)

    with ExitStack() as ctx:
        keep = ctx.enter_context(tc.tile_pool(name="keep", bufs=1))
        work = ctx.enter_context(tc.tile_pool(name="work", bufs=4))
        psum = ctx.enter_context(tc.psum_pool(name="psum", bufs=1))
        ctx.enter_context(tc.manual_schedule())

        ident_f32 = keep.tile([P, P], F32, name="ident_f32")
        ident_bf16 = keep.tile([P, P], BF16, name="ident_bf16")
        vectors = keep.tile([P, D], BF16, name="vectors")
        trig = keep.tile([P, 4, 2, D // 2], BF16, name="trig")
        spread = keep.tile([P, 2 * D + NORMED], F32, name="spread")
        bv_rows = keep.tile([P, BLOCK], BF16, name="bv_rows")
        x_sb = [keep.tile([P, TILES, K_PASS], BF16, name="x_%d" % g) for g in range(PASSES)]
        x_grouped = [keep.tile([P, TOKENS, 4], BF16, name="xg_%d" % g, align_bytes=64) for g in range(PASSES)]
        x_codes = [keep.tile([P, TOKENS], U32, name="xc_%d" % g, align_bytes=64) for g in range(PASSES)]
        x_scales = [keep.tile([P, TOKENS], U8, name="xs_%d" % g, align_bytes=64) for g in range(PASSES)]
        words = {
            first: keep.tile([P, PASSES, 2 * D * count], U8, name="words_%d" % first, align_bytes=64)
            for first, count in WORD_LOADS
        }
        plane_first = keep.tile([P, PASSES, BLOCK], U8, name="plane_first", align_bytes=64)
        plane_rest = keep.tile([P, PASSES, 3 * BLOCK], U8, name="plane_rest", align_bytes=64)
        plane_k = keep.tile([P, PASSES, BLOCK], U8, name="plane_k", align_bytes=64)
        plane_v = keep.tile([P, PASSES, BLOCK], U8, name="plane_v", align_bytes=64)
        tables = [keep.tile([P, 2, D, 2], F32, name="table_%d" % n) for n in range(2)]

        def zero_plane(plane):
            filler = plane[:].rearrange("p g n -> p (g n)").bitcast(I32)
            cut = filler.shape[1] // 2 + 1
            nc.vector.memset(filler[:, 0:cut], 0)
            nc.vector.memset(filler[:, cut:], 0)

        def load_x(g):
            for a in range(2):
                tiles = slice(2 * a, 2 * a + 2)
                nc.sync.dma_start(out=x_sb[g][:, tiles, :], in_=x_rows[:, tiles, K_PASS * g : K_PASS * (g + 1)])

        def load_scales(plane, scales):
            for q in range(4):
                nc.sync.dma_start(
                    out=plane[32 * q : 32 * q + 4, :, :].bitcast(I32),
                    in_=scales[:, 4 * q : 4 * q + 4, :].rearrange("g r n -> r g n").bitcast(I32),
                )

        def load_words(first, src):
            nc.sync.dma_start(out=words[first][:].bitcast(I32), in_=src.rearrange("g p n -> p g n").bitcast(I32))

        def load_q_words(first, count):
            load_words(first, Wq_words[:, :, 2 * D * first : 2 * D * (first + count)])

        zero_plane(plane_first)
        make_identity(nc, ident_f32[:])
        table_preload = keep.tile([P, 1], F32, name="table_preload")
        nc.scalar.activation(out=table_preload[:], in_=ident_f32[:, 0:1], func=ACT.Abs_reciprocal_sqrt, bias=1.0)
        nc.gpsimd.memset(vectors[:], 0.0)
        nc.gpsimd.dma_start(out=vectors[0:H, :], in_=bq.rearrange("(h d) -> h d", d=D))
        nc.gpsimd.dma_start(out=vectors[H:NORMED, :], in_=bk.rearrange("(h d) -> h d", d=D))
        nc.gpsimd.dma_start(out=vectors[NORMED : NORMED + 1, :], in_=qn_w.rearrange("(o d) -> o d", o=1))
        nc.gpsimd.dma_start(out=vectors[NORMED + 1 : NORMED + 2, :], in_=kn_w.rearrange("(o d) -> o d", o=1))
        nc.gpsimd.dma_start(out=trig[:, 0, :, :], in_=freqs_cos.rearrange("(u p) j -> p u j", p=P))
        nc.gpsimd.dma_start(out=trig[:, 1, :, :], in_=freqs_sin.rearrange("(u p) j -> p u j", p=P))
        zero_plane(plane_rest)
        nc.vector.tensor_copy(out=ident_bf16[:], in_=ident_f32[:])

        load_x(0)
        load_scales(plane_first, Wq_scales[:, :, 0:BLOCK])
        load_x(1)
        load_q_words(0, 2)
        for g in range(2, PASSES):
            load_x(g)
        load_q_words(2, 2)
        load_scales(plane_rest, Wq_scales[:, :, BLOCK : 4 * BLOCK])
        load_q_words(4, 4)
        load_q_words(8, 4)

        def turn_x(g):
            banks = []
            for a in range(2):
                bank = psum.tile([P, 2, 2, P], F32, name="xt", tag="turn%d" % ((2 * g + a) % BANKS))
                pairs = x_sb[g][:, 2 * a : 2 * a + 2, :].rearrange("p i k -> p (i k)").bitcast(F32)
                for i in range(2):
                    for u in range(2):
                        nc.tensor.transpose(bank[:, i, u, :], pairs[:, 256 * i + u : 256 * (i + 1) : 2], ident_f32[:])
                banks.append(bank)
            return banks

        def quantize_x(g, banks):
            halves = []
            for a in range(2):
                half = x_grouped[g][:, 256 * a : 256 * (a + 1), :].rearrange("p r t -> p (r t)")
                halves.append(half)
                dst = half.bitcast(F32).rearrange("p (i r u) -> p i r u", i=2, u=2)
                src = banks[a][:].rearrange("p i u r -> p i r u")
                if a == 0:
                    nc.vector.tensor_copy(out=dst, in_=src)
                else:
                    nc.scalar.copy(out=dst, in_=src)
            for a in range(2):
                cols = slice(256 * a, 256 * (a + 1))
                nc.vector.quantize_mx(out=x_codes[g][:, cols].bitcast(E5M2X4), scales=x_scales[g][:, cols], in_=halves[a])

        def head_plane(h, g):
            j, c = divmod(h, HEADS_PER_BLOCK)
            if j == 0:
                return plane_first[:, g, D * c : D * (c + 1)]
            if j == 4:
                return plane_k[:, g, D * c : D * (c + 1)]
            return plane_rest[:, g, D * (h - HEADS_PER_BLOCK) : D * (h - HEADS_PER_BLOCK + 1)]

        sums = {}
        biased = {}
        turned = {}
        squares = {}
        inverse = {}

        def project_pass(h, g):
            if g == 0:
                sums[h] = psum.tile([P, TOKENS], F32, name="sums", tag="sum%d" % (h % BANKS))
            first = max(f for f, count in WORD_LOADS if f <= h)
            c = h - first
            nc.tensor.matmul_mx(
                out=sums[h][:],
                lhsT=words[first][:, g, 2 * D * c : 2 * D * (c + 1)].bitcast(E2M1X4),
                lhsT_scale=head_plane(h, g),
                rhs=x_codes[g][:].bitcast(E5M2X4),
                rhs_scale=x_scales[g][:],
                start=(g == 0),
                stop=(g == PASSES - 1),
            )

        def add_bias(h):
            biased[h] = work.tile([P, TOKENS], F32, name="biased")
            bias = spread[:, 2 * D + h : 2 * D + h + 1]
            if h % 2 == 0 and OPEN_AT_START < h < H:
                nc.vector.tensor_scalar(out=biased[h][:], in0=sums[h][:], scalar1=bias, scalar2=None, op0=ALU.add)
            else:
                nc.scalar.activation(out=biased[h][:], in_=sums[h][:], func=ACT.Identity, bias=bias)

        def project(h):
            for g in range(PASSES):
                project_pass(h, g)
            add_bias(h)

        def turn_head(h):
            turned[h] = psum.tile([P, TILES, D], F32, name="turned", tag="turn%d" % (h % BANKS))
            for i in range(TILES):
                nc.tensor.transpose(turned[h][:, i, :], biased[h][:, P * i : P * (i + 1)], ident_f32[:])

        def sum_squares(h, tiles):
            if h not in squares:
                squares[h] = work.tile([P, TILES], F32, name="squares")
            for i in tiles:
                unread = work.tile([P, D], BF16, name="unread")
                nc.scalar.activation(out=unread[:], in_=turned[h][:, i, :], func=ACT.Square, accum_out=squares[h][:, i : i + 1])

        def invert(h):
            inverse[h] = work.tile([P, TILES], F32, name="inverse")
            nc.scalar.activation(out=inverse[h][:], in_=squares[h][:], func=ACT.Abs_reciprocal_sqrt, scale=1.0 / D, bias=EPS)

        def multiply(h, terms):
            table = tables[0 if h < H else 1]
            for i in range(TILES):
                nc.vector.scalar_tensor_tensor(
                    out=terms[:, i, h % 2, :, :],
                    in0=table[:, i % 2, :, :],
                    scalar=inverse[h][:, i : i + 1],
                    in1=turned[h][:, i, :].unsqueeze(2).to_broadcast([P, D, 2]),
                    op0=ALU.mult,
                    op1=ALU.mult,
                )

        def add_and_store(first, count, terms, rotated):
            heads = slice(first % 2, first % 2 + count)
            by_pair = terms[:, :, heads, :, :].rearrange("p i n (j e) c -> p i (n j) e c", e=2)
            result = rotated[:, :, heads, :].rearrange("p i n d -> p i (n d)")
            nc.gpsimd.tensor_tensor(
                out=result.rearrange("p i (j c) -> p i j c", c=2),
                in0=by_pair[:, :, :, 0, :],
                in1=by_pair[:, :, :, 1, :],
                op=ALU.add,
            )
            rows, col = (q_rows, D * first) if first < H else (k_rows, D * (first - H))
            nc.sync.dma_start(out=rows[:, :, col : col + D * count], in_=result)

        def rotate_pair(h):
            terms = work.tile([P, TILES, 2, D, 2], F32, name="terms", bufs=3)
            rotated = work.tile([P, TILES, 2, D], F32, name="rotated")
            if h < H:
                multiply(h, terms)
                multiply(h + 1, terms)
                add_and_store(h, 2, terms, rotated)
            else:
                for n in (h, h + 1):
                    multiply(n, terms)
                    add_and_store(n, 1, terms, rotated)

        def project_v(i):
            acc = psum.tile([P, BLOCK], F32, name="acc_v", tag="sum%d" % ((NORMED + i) % BANKS))
            for g in range(PASSES):
                nc.tensor.matmul_mx(
                    out=acc[:],
                    lhsT=x_codes[g][:, P * i : P * (i + 1)].bitcast(E5M2X4),
                    lhsT_scale=x_scales[g][:, P * i : P * (i + 1)],
                    rhs=words[NORMED][:, g, :].bitcast(E2M1X4),
                    rhs_scale=plane_v[:, g, :],
                    start=(g == 0),
                    stop=(g == PASSES - 1),
                )
            return acc

        def finish_v(i, acc):
            result = work.tile([P, BLOCK], F32, name="result_v")
            nc.vector.tensor_tensor(out=result[:], in0=bv_rows[:], in1=acc[:], op=ALU.add)
            nc.sync.dma_start(out=v_rows[:, i, :], in_=result[:])

        def spread_vectors():
            bank = psum.tile([P, 2 * D + 32], F32, name="spread_bank", tag="sum%d" % (BANKS - 1))
            nc.tensor.matmul(bank[:, 2 * D : 2 * D + 32], lhsT=vectors[:], rhs=ident_bf16[:, 0:32], start=True, stop=True)
            for n in range(2):
                row = NORMED + n
                nc.tensor.matmul(
                    bank[:, D * n : D * (n + 1)], lhsT=ident_bf16[:, row : row + 1].to_broadcast([P, P]),
                    rhs=vectors[:], start=True, stop=True,
                )
            nc.scalar.copy(out=spread[:], in_=bank[:, 0 : 2 * D + NORMED])

        def build_table(n):
            gain = spread[:, D * n : D * (n + 1)].rearrange("p (j e o) -> p j e o", e=2, o=1)
            for u in range(2):
                nc.vector.tensor_tensor(
                    out=tables[n][:, u, :, :].rearrange("p (j e) c -> p j e c", e=2),
                    in0=trig[:, :, u, :].rearrange("p (e c) j -> p j e c", e=2),
                    in1=gain.to_broadcast([P, D // 2, 2, 2]),
                    op=ALU.mult,
                )

        quantize_x(0, turn_x(0))
        for g in range(PASSES):
            if g + 1 < PASSES:
                quantize_x(g + 1, turn_x(g + 1))
            for h in range(OPEN_AT_START):
                project_pass(h, g)
            if g + 2 == PASSES:
                spread_vectors()
                nc.vector.tensor_scalar(out=trig[:, 2, :, :], in0=trig[:, 1, :, :], scalar1=-1.0, scalar2=None, op0=ALU.mult)
                nc.vector.tensor_copy(out=trig[:, 3, :, :], in_=trig[:, 0, :, :])
                build_table(0)
                build_table(1)
        zero_plane(plane_k)
        zero_plane(plane_v)
        load_scales(plane_k, Wk_scales)
        load_scales(plane_v, Wv_scales)
        load_q_words(12, 4)
        load_words(H, Wk_words)
        load_words(NORMED, Wv_words)
        for h in range(OPEN_AT_START):
            add_bias(h)

        project(OPEN_AT_START)
        for h in range(0, NORMED, 2):
            turn_head(h)
            turn_head(h + 1)
            sum_squares(h, range(TILES))
            sum_squares(h + 1, range(1))
            invert(h)
            sum_squares(h + 1, range(1, TILES))
            if h + 3 < NORMED:
                project(h + 3)
            invert(h + 1)
            rotate_pair(h)
            if h == H // 2:
                nc.sync.dma_start(out=bv_rows[:], in_=bv.partition_broadcast(P))
            if h + 4 < NORMED:
                project(h + 4)
            if h + 4 == NORMED:
                finish_v(0, project_v(0))
        for i in range(1, TILES):
            finish_v(i, project_v(i))
